import numpy as np
import ml_dtypes


def mxq(x, axis, fmt="e4m3"):
    dtype, down = {"e4m3": (ml_dtypes.float8_e4m3fn, 7), "e5m2": (ml_dtypes.float8_e5m2, 14)}[fmt]
    v = np.moveaxis(np.asarray(x, np.float32).astype(ml_dtypes.bfloat16).astype(np.float64), axis, -1)
    blocks = v.reshape(v.shape[:-1] + (-1, 32))
    amax = np.abs(blocks).max(-1, keepdims=True)
    byte = np.maximum(np.where(amax > 0, np.frexp(amax)[1] - 1 + 127, 0) - down, 1)
    scale = np.exp2(byte - 127.0)
    codes = (blocks / scale).astype(np.float32).astype(dtype).astype(np.float64)
    return np.moveaxis((codes * scale).reshape(v.shape), -1, axis)


WIDE = False


def mx_kscale(k):
    if not WIDE:
        return np.ones(k)
    levels = np.array([10, -10, 5, -5, 0])
    a = np.random.permutation(np.resize(levels, k // 512 * 4)).reshape(k // 512, 4)
    idx = np.arange(k)
    return np.exp2(a[idx // 512, idx % 128 // 32])


BF16 = ml_dtypes.bfloat16


def bf(x):
    return np.asarray(x, np.float32).astype(BF16)


def f64(x):
    return np.asarray(x).astype(np.float64)


B, IN_C, OUT_C, H, W, K, STRIDE, PAD = 512, 512, 128, 4, 4, 3, 1, 1
OH = (H + 2 * PAD - K) // STRIDE + 1
OW = (W + 2 * PAD - K) // STRIDE + 1


def _span(t, n_in, n_out):
    lo = max(0, -((t - PAD) // STRIDE))
    hi = min(n_out, (n_in - 1 + PAD - t) // STRIDE + 1)
    return lo, hi


def setup_inputs():
    s = mx_kscale(IN_C)
    x = np.random.standard_normal((B, IN_C, H, W)) * s[None, :, None, None]
    weights = np.random.uniform(0.0, 1.0, (OH, OW, OUT_C, IN_C, K, K)) * (1.7 / np.sqrt(IN_C * K * K)) / s[None, None, None, :, None, None]
    bias = np.random.uniform(0.0, 1.0, (OUT_C, OH, OW))
    return {"x": bf(x), "weights": bf(weights), "bias": bf(bias)}


def reference(x, weights, bias):
    xq = mxq(f64(x), 1, "e4m3")
    wf = f64(weights)
    acc = np.zeros((OH, OW, B, OUT_C))
    for i in range(K):
        h0, h1 = _span(i, H, OH)
        for j in range(K):
            w0, w1 = _span(j, W, OW)
            xs = xq[:, :, h0 * STRIDE + i - PAD:(h1 - 1) * STRIDE + i - PAD + 1:STRIDE,
                    w0 * STRIDE + j - PAD:(w1 - 1) * STRIDE + j - PAD + 1:STRIDE]
            wq = mxq(wf[h0:h1, w0:w1, :, :, i, j], 3, "e4m3")
            acc[h0:h1, w0:w1] += xs.transpose(2, 3, 0, 1) @ wq.transpose(0, 1, 3, 2)
    return acc.transpose(2, 3, 0, 1) + f64(bias)[None]

@@ -1,0 +1,214 @@
+from contextlib import ExitStack
+
+import concourse.mybir as mybir
+from concourse.masks import make_identity
+
+BF16 = mybir.dt.bfloat16
+F32 = mybir.dt.float32
+U32 = mybir.dt.uint32
+U8 = mybir.dt.uint8
+FP8X4 = mybir.dt.float8_e4m3fn_x4
+
+P = 128
+B, C, O, H, W, KK = 512, 512, 128, 4, 4, 3
+S = H * W
+TAPS = KK * KK
+NBT = B // P
+UNIT = 512
+UW = 128
+RUN = 8
+
+N_VALID = 100
+FLOPS = 2 * B * O * C * N_VALID
+BYTES = B * C * S * 2 + N_VALID * O * C * 2 + O * S * 2 + B * O * S * 4
+
+XBUFS = 8
+WBUFS = 5
+
+
+def valid_taps(h, w):
+    return [(i, j) for i in range(KK) for j in range(KK)
+            if 0 <= h + i - 1 < H and 0 <= w + j - 1 < W]
+
+
+def tile_locallyconnected2d_t_kernel(tc, x, weights, bias, out):
+    nc = tc.nc
+    x_rows = x.rearrange("b (q c) h w -> (b q) (c h w)", q=4).rearrange("(a p) e -> a p e", p=P)
+    w_rows = weights.rearrange("h w o (q c) i j -> (h w) (o q) (c i j)", q=4).rearrange(
+        "g (a p) e -> g p a e", p=P)
+    out_rows = out.rearrange("(t p) o h w -> t p (o h w)", p=P)
+    n_chunks = x_rows.shape[0]
+
+    with ExitStack() as ctx:
+        const = ctx.enter_context(tc.tile_pool(name="const", bufs=1))
+        xraw_pool = ctx.enter_context(tc.tile_pool(name="xraw", bufs=XBUFS))
+        wraw_pool = ctx.enter_context(tc.tile_pool(name="wraw", bufs=WBUFS))
+        stage_pool = ctx.enter_context(tc.tile_pool(name="stage", bufs=4))
+        wq_pool = ctx.enter_context(tc.tile_pool(name="wq", bufs=5))
+        tp_pool = ctx.enter_context(tc.psum_pool(name="tp", bufs=4))
+        acc_pool = ctx.enter_context(tc.psum_pool(name="acc", bufs=1))
+        ctx.enter_context(tc.manual_schedule())
+
+        ident = const.tile([P, P], BF16, name="ident")
+        make_identity(nc, ident[:])
+        x_codes = const.tile([P, NBT * S * UW], U32, name="x_codes", align_bytes=64)
+        x_scales = const.tile([P, NBT * S * UW], U8, name="x_scales", align_bytes=64)
+        bias_sb = const.tile([P, O * S], BF16, name="bias_sb")
+        out_sb = [const.tile([P, O * S], F32, name="out_sb%d" % t) for t in range(NBT)]
+
+        state = {"bank": 0}
+
+        def leave_psum(dst, src):
+            k = state["bank"]
+            state["bank"] = k + 1
+            if k % 4 == 1:
+                nc.vector.tensor_copy(out=dst, in_=src)
+            else:
+                nc.scalar.copy(out=dst, in_=src)
+
+        def quantise(codes, scales, stage, u0, n, c0):
+            nc.vector.quantize_mx(
+                out=codes[:, c0:c0 + n * UW].bitcast(FP8X4),
+                scales=scales[:, c0:c0 + n * UW],
+                in_=stage[:, u0 * UNIT:(u0 + n) * UNIT],
+            )
+
+        xraw = {}
+        wraw = {}
+
+        def load_x(a):
+            t = xraw_pool.tile([P, C // 4 * S], BF16, name="xraw%d" % a, tag="xraw")
+            nc.sync.dma_start(out=t[:], in_=x_rows[a])
+            xraw[a] = t
+
+        def load_w(g):
+            t = wraw_pool.tile([P, 4, C // 4 * TAPS], BF16, name="wraw%d" % g, tag="wraw")
+            nc.sync.dma_start(out=t[:], in_=w_rows[g])
+            wraw[g] = t
+
+        for a in range(XBUFS):
+            load_x(a)
+
+        pending = []
+        xstage = {}
+        for a in range(n_chunks):
+            bt, al = a // 4, a % 4
+            view = xraw[a].rearrange("p (c s) -> p c s", s=S)
+            for half in range(2):
+                if al == 0:
+                    xstage[half] = stage_pool.tile([P, RUN * UNIT], BF16, name="xst%d_%d" % (bt, half),
+                                                   tag="stage", align_bytes=64)
+                bank = tp_pool.tile([P, 2 * UNIT], BF16, name="xtp%d_%d" % (a, half), tag="tp")
+                for k in range(8):
+                    nc.tensor.transpose(bank[:, k * P:(k + 1) * P], view[:, :, 8 * half + k], ident[:])
+                leave_psum(
+                    xstage[half].rearrange("p (s a n) -> p s a n", s=8, a=4)[:, :, al, :],
+                    bank.rearrange("p (s n) -> p s n", s=8),
+                )
+            for job in pending:
+                quantise(*job)
+            pending = []
+            if al == 3:
+                for half in range(2):
+                    pending.append((x_codes, x_scales, xstage[half], 0, 8, (bt * S + 8 * half) * UW))
+            if a + XBUFS < n_chunks:
+                load_x(a + XBUFS)
+            elif a + XBUFS == n_chunks:
+                for g in range(WBUFS):
+                    load_w(g)
+                    if g == 1:
+                        nc.sync.dma_start(
+                            out=bias_sb[:],
+                            in_=bias.rearrange("o h w -> (o h w)").partition_broadcast(P))
+
+        runs = []
+        for h in range(H):
+            row = []
+            for w in range(W):
+                taps = valid_taps(h, w)
+                for n, (i, j) in enumerate(taps):
+                    row.append((h, w, i, j, n == 0, n == len(taps) - 1))
+            for r0 in range(0, len(row), RUN):
+                runs.append((h, row[r0:r0 + RUN]))
+        last_use = {}
+        for r, (h, units) in enumerate(runs):
+            for u in units:
+                last_use[u[0] * W + u[1]] = r
+
+        wq = {}
+        acc = {}
+
+        def transposes(r):
+            h, units = runs[r]
+            n = len(units)
+            stage = stage_pool.tile([P, RUN * UNIT], BF16, name="wst%d" % r, tag="stage", align_bytes=64)
+            for k in range(0, n, 2):
+                bank = tp_pool.tile([P, 2 * UNIT], BF16, name="wtp%d_%d" % (r, k), tag="tp")
+                for e in range(2):
+                    uh, uw, i, j = units[k + e][:4]
+                    view = wraw[uh * W + uw].rearrange("p a (c t) -> p a c t", t=TAPS)
+                    for a in range(4):
+                        c0 = e * UNIT + a * P
+                        nc.tensor.transpose(bank[:, c0:c0 + P], view[:, a, :, i * KK + j], ident[:])
+                leave_psum(stage[:, k * UNIT:(k + 2) * UNIT], bank[:])
+            for job in pending:
+                quantise(*job)
+            codes = wq_pool.tile([P, RUN * UW], U32, name="wc%d" % r, tag="wc", align_bytes=64)
+            scales = wq_pool.tile([P, RUN * UW], U8, name="ws%d" % r, tag="ws", align_bytes=64)
+            u0 = 0
+            for width in (8, 4, 2):
+                if n - u0 >= width:
+                    quantise(codes, scales, stage, u0, width, u0 * UW)
+                    u0 += width
+            wq[r] = (codes, scales)
+            for g in range(S):
+                if last_use[g] == r and g + WBUFS < S:
+                    load_w(g + WBUFS)
+
+        def passes(h, bt, todo):
+            if (h, bt) not in acc:
+                acc[(h, bt)] = acc_pool.tile([P, W * O], F32, name="acc%d_%d" % (h, bt), tag="acc%d" % bt)
+            bank = acc[(h, bt)]
+            for r, k, (uh, uw, i, j, first, last) in todo:
+                codes, scales = wq[r]
+                s = (uh + i - 1) * W + (uw + j - 1)
+                xc = (bt * S + s) * UW
+                nc.tensor.matmul_mx(
+                    out=bank[:, uw * O:(uw + 1) * O],
+                    lhsT=x_codes[:, xc:xc + UW].bitcast(FP8X4),
+                    lhsT_scale=x_scales[:, xc:xc + UW],
+                    rhs=codes[:, k * UW:(k + 1) * UW].bitcast(FP8X4),
+                    rhs_scale=scales[:, k * UW:(k + 1) * UW],
+                    start=first,
+                    stop=last,
+                )
+
+        def finish(h, bt):
+            nc.vector.tensor_tensor(
+                out=out_sb[bt].rearrange("p (o s) -> p o s", s=S)[:, :, h * W:(h + 1) * W],
+                in0=acc[(h, bt)].rearrange("p (w o) -> p o w", w=W),
+                in1=bias_sb.rearrange("p (o s) -> p o s", s=S)[:, :, h * W:(h + 1) * W],
+                op=mybir.AluOpType.add,
+            )
+
+        def multiply(r):
+            h, units = runs[r]
+            closes = r + 1 == len(runs) or runs[r + 1][0] != h
+            todo = [(r, k, u) for k, u in enumerate(units)]
+            for bt in range(NBT):
+                passes(h, bt, todo)
+                if closes:
+                    finish(h, bt)
+
+        for r in range(len(runs)):
+            transposes(r)
+            pending = []
+            if r >= 1 and runs[r - 1][0] != H - 1:
+                multiply(r - 1)
+
+        todo = [(r, k, u) for r in range(len(runs)) if runs[r][0] == H - 1
+                for k, u in enumerate(runs[r][1])]
+        for bt in range(NBT):
+            passes(H - 1, bt, todo)
+            finish(H - 1, bt)
+            nc.sync.dma_start(out=out_rows[bt], in_=out_sb[bt][:])

@@ -22,8 +22,10 @@ N_VALID = 100
 FLOPS = 2 * B * O * C * N_VALID
 BYTES = B * C * S * 2 + N_VALID * O * C * 2 + O * S * 2 + B * O * S * 4
 
-XBUFS = 8
-WBUFS = 5
+XBUFS = 4
+WBUFS = 4
+SORT_ON_SCALAR = 4
+AHEAD = 2
 
 
 def valid_taps(h, w):
@@ -33,8 +35,8 @@ def valid_taps(h, w):
 
 def tile_locallyconnected2d_t_kernel(tc, x, weights, bias, out):
     nc = tc.nc
-    x_rows = x.rearrange("b (q c) h w -> (b q) (c h w)", q=4).rearrange("(a p) e -> a p e", p=P)
-    w_rows = weights.rearrange("h w o (q c) i j -> (h w) (o q) (c i j)", q=4).rearrange(
+    x_rows = x.rearrange("b (z c) h w -> (b z) (c h w)", z=2).rearrange("(a p) e -> a p e", p=P)
+    w_rows = weights.rearrange("h w o (z c) i j -> (h w) (o z) (c i j)", z=2).rearrange(
         "g (a p) e -> g p a e", p=P)
     out_rows = out.rearrange("(t p) o h w -> t p (o h w)", p=P)
     n_chunks = x_rows.shape[0]
@@ -43,28 +45,20 @@ def tile_locallyconnected2d_t_kernel(tc, x, weights, bias, out):
         const = ctx.enter_context(tc.tile_pool(name="const", bufs=1))
         xraw_pool = ctx.enter_context(tc.tile_pool(name="xraw", bufs=XBUFS))
         wraw_pool = ctx.enter_context(tc.tile_pool(name="wraw", bufs=WBUFS))
-        stage_pool = ctx.enter_context(tc.tile_pool(name="stage", bufs=4))
-        wq_pool = ctx.enter_context(tc.tile_pool(name="wq", bufs=5))
+        work_pool = ctx.enter_context(tc.tile_pool(name="work", bufs=7))
+        wq_pool = ctx.enter_context(tc.tile_pool(name="wq", bufs=4))
         tp_pool = ctx.enter_context(tc.psum_pool(name="tp", bufs=4))
         acc_pool = ctx.enter_context(tc.psum_pool(name="acc", bufs=1))
         ctx.enter_context(tc.manual_schedule())
 
-        ident = const.tile([P, P], BF16, name="ident")
+        ident = const.tile([P, P], F32, name="ident")
         make_identity(nc, ident[:])
         x_codes = const.tile([P, NBT * S * UW], U32, name="x_codes", align_bytes=64)
         x_scales = const.tile([P, NBT * S * UW], U8, name="x_scales", align_bytes=64)
         bias_sb = const.tile([P, O * S], BF16, name="bias_sb")
         out_sb = [const.tile([P, O * S], F32, name="out_sb%d" % t) for t in range(NBT)]
 
-        state = {"bank": 0}
-
-        def leave_psum(dst, src):
-            k = state["bank"]
-            state["bank"] = k + 1
-            if k % 4 == 1:
-                nc.vector.tensor_copy(out=dst, in_=src)
-            else:
-                nc.scalar.copy(out=dst, in_=src)
+        state = {"xbank": 0, "sort": 0}
 
         def quantise(codes, scales, stage, u0, n, c0):
             nc.vector.quantize_mx(
@@ -72,54 +66,6 @@ def tile_locallyconnected2d_t_kernel(tc, x, weights, bias, out):
                 scales=scales[:, c0:c0 + n * UW],
                 in_=stage[:, u0 * UNIT:(u0 + n) * UNIT],
             )
-
-        xraw = {}
-        wraw = {}
-
-        def load_x(a):
-            t = xraw_pool.tile([P, C // 4 * S], BF16, name="xraw%d" % a, tag="xraw")
-            nc.sync.dma_start(out=t[:], in_=x_rows[a])
-            xraw[a] = t
-
-        def load_w(g):
-            t = wraw_pool.tile([P, 4, C // 4 * TAPS], BF16, name="wraw%d" % g, tag="wraw")
-            nc.sync.dma_start(out=t[:], in_=w_rows[g])
-            wraw[g] = t
-
-        for a in range(XBUFS):
-            load_x(a)
-
-        pending = []
-        xstage = {}
-        for a in range(n_chunks):
-            bt, al = a // 4, a % 4
-            view = xraw[a].rearrange("p (c s) -> p c s", s=S)
-            for half in range(2):
-                if al == 0:
-                    xstage[half] = stage_pool.tile([P, RUN * UNIT], BF16, name="xst%d_%d" % (bt, half),
-                                                   tag="stage", align_bytes=64)
-                bank = tp_pool.tile([P, 2 * UNIT], BF16, name="xtp%d_%d" % (a, half), tag="tp")
-                for k in range(8):
-                    nc.tensor.transpose(bank[:, k * P:(k + 1) * P], view[:, :, 8 * half + k], ident[:])
-                leave_psum(
-                    xstage[half].rearrange("p (s a n) -> p s a n", s=8, a=4)[:, :, al, :],
-                    bank.rearrange("p (s n) -> p s n", s=8),
-                )
-            for job in pending:
-                quantise(*job)
-            pending = []
-            if al == 3:
-                for half in range(2):
-                    pending.append((x_codes, x_scales, xstage[half], 0, 8, (bt * S + 8 * half) * UW))
-            if a + XBUFS < n_chunks:
-                load_x(a + XBUFS)
-            elif a + XBUFS == n_chunks:
-                for g in range(WBUFS):
-                    load_w(g)
-                    if g == 1:
-                        nc.sync.dma_start(
-                            out=bias_sb[:],
-                            in_=bias.rearrange("o h w -> (o h w)").partition_broadcast(P))
 
         runs = []
         for h in range(H):
@@ -135,24 +81,110 @@ def tile_locallyconnected2d_t_kernel(tc, x, weights, bias, out):
             for u in units:
                 last_use[u[0] * W + u[1]] = r
 
+        xraw = {}
+        wraw = {}
+
+        def load_x(a):
+            t = xraw_pool.tile([P, C // 2 * S], BF16, name="xraw%d" % a, tag="xraw")
+            nc.sync.dma_start(out=t[:], in_=x_rows[a])
+            xraw[a] = t
+
+        def load_w(g):
+            t = wraw_pool.tile([P, 2, C // 2 * TAPS], BF16, name="wraw%d" % g, tag="wraw")
+            nc.sync.dma_start(out=t[:], in_=w_rows[g])
+            wraw[g] = t
+
+        sorted_w = {}
+
+        def sort_taps(r):
+            h, units = runs[r]
+            dst = work_pool.tile([P, RUN * UNIT], BF16, name="srt%d" % r, tag="work", align_bytes=64)
+            dst_v = dst.rearrange("p (k c) -> p c k", c=UNIT)
+            k = 0
+            while k < len(units):
+                uh, uw, i, j = units[k][:4]
+                n = 1
+                while k + n < len(units) and units[k + n][:3] == (uh, uw, i):
+                    n += 1
+                src_v = wraw[uh * W + uw].rearrange("p g (c t) -> p (g c) t", t=TAPS)
+                t0 = i * KK + j
+                cnt = state["sort"]
+                state["sort"] = cnt + 1
+                if cnt % SORT_ON_SCALAR == SORT_ON_SCALAR - 1:
+                    nc.scalar.copy(out=dst_v[:, :, k:k + n], in_=src_v[:, :, t0:t0 + n])
+                else:
+                    nc.vector.tensor_copy(out=dst_v[:, :, k:k + n], in_=src_v[:, :, t0:t0 + n])
+                k += n
+            sorted_w[r] = dst
+            for g in range(S):
+                if last_use[g] == r and g + WBUFS < S:
+                    load_w(g + WBUFS)
+
+        for a in range(XBUFS):
+            load_x(a)
+
+        pending = []
+        xstage = {}
+        for a in range(n_chunks):
+            bt, ah = a // 2, a % 2
+            words = xraw[a].bitcast(F32).rearrange("p (m k) -> p m k", k=S)
+            for q in range(4):
+                half, u0 = q // 2, (4 * q) % 8
+                if ah == 0 and u0 == 0:
+                    xstage[half] = work_pool.tile([P, RUN * UNIT], BF16, name="xst%d_%d" % (bt, half),
+                                                  tag="work", align_bytes=64)
+                bank = tp_pool.tile([P, UNIT], F32, name="xtp%d_%d" % (a, q), tag="tp")
+                for l in range(2):
+                    for e in range(2):
+                        c0 = (2 * l + e) * P
+                        nc.tensor.transpose(bank[:, c0:c0 + P], words[:, :, 8 * e + 2 * q + l], ident[:])
+                src = bank.bitcast(BF16).rearrange("p (l e n g) -> p l g n e", l=2, e=2, g=2)
+                dst = xstage[half].rearrange("p (u a n e) -> p u a n e", u=8, a=2, e=2)
+                k = state["xbank"]
+                state["xbank"] = k + 1
+                for l in range(2):
+                    if k % 5 in (1, 3):
+                        nc.vector.tensor_copy(out=dst[:, u0 + 2 * l:u0 + 2 * l + 2, ah, :, :], in_=src[:, l])
+                    else:
+                        nc.scalar.copy(out=dst[:, u0 + 2 * l:u0 + 2 * l + 2, ah, :, :], in_=src[:, l])
+            for job in pending:
+                quantise(*job)
+            pending = []
+            if ah == 1:
+                for half in range(2):
+                    pending.append((x_codes, x_scales, xstage[half], 0, 8, (bt * S + 8 * half) * UW))
+            if a + XBUFS < n_chunks:
+                load_x(a + XBUFS)
+            elif a + XBUFS == n_chunks:
+                for g in range(WBUFS):
+                    load_w(g)
+                    if g == 1:
+                        nc.sync.dma_start(
+                            out=bias_sb[:],
+                            in_=bias.rearrange("o h w -> (o h w)").partition_broadcast(P))
+
+        sort_taps(0)
+        for job in pending:
+            quantise(*job)
+        sort_taps(1)
+
         wq = {}
         acc = {}
 
         def transposes(r):
             h, units = runs[r]
             n = len(units)
-            stage = stage_pool.tile([P, RUN * UNIT], BF16, name="wst%d" % r, tag="stage", align_bytes=64)
+            stage = work_pool.tile([P, RUN * UNIT], BF16, name="wst%d" % r, tag="work", align_bytes=64)
+            words = sorted_w[r].bitcast(F32)
+            stage_w = stage.bitcast(F32)
             for k in range(0, n, 2):
-                bank = tp_pool.tile([P, 2 * UNIT], BF16, name="wtp%d_%d" % (r, k), tag="tp")
-                for e in range(2):
-                    uh, uw, i, j = units[k + e][:4]
-                    view = wraw[uh * W + uw].rearrange("p a (c t) -> p a c t", t=TAPS)
-                    for a in range(4):
-                        c0 = e * UNIT + a * P
-                        nc.tensor.transpose(bank[:, c0:c0 + P], view[:, a, :, i * KK + j], ident[:])
-                leave_psum(stage[:, k * UNIT:(k + 2) * UNIT], bank[:])
-            for job in pending:
-                quantise(*job)
+                bank = tp_pool.tile([P, UNIT], F32, name="wtp%d_%d" % (r, k), tag="tp")
+                for e in range(4):
+                    c0 = (2 * k + e) * P
+                    nc.tensor.transpose(bank[:, e * P:(e + 1) * P], words[:, c0:c0 + P], ident[:])
+                nc.scalar.copy(out=stage_w[:, k * 256:(k + 2) * 256], in_=bank[:])
+            if r + AHEAD < len(runs):
+                sort_taps(r + AHEAD)
             codes = wq_pool.tile([P, RUN * UW], U32, name="wc%d" % r, tag="wc", align_bytes=64)
             scales = wq_pool.tile([P, RUN * UW], U8, name="ws%d" % r, tag="ws", align_bytes=64)
             u0 = 0
@@ -161,9 +193,6 @@ def tile_locallyconnected2d_t_kernel(tc, x, weights, bias, out):
                     quantise(codes, scales, stage, u0, width, u0 * UW)
                     u0 += width
             wq[r] = (codes, scales)
-            for g in range(S):
-                if last_use[g] == r and g + WBUFS < S:
-                    load_w(g + WBUFS)
 
         def passes(h, bt, todo):
             if (h, bt) not in acc:
@@ -202,7 +231,6 @@ def tile_locallyconnected2d_t_kernel(tc, x, weights, bias, out):
 
         for r in range(len(runs)):
             transposes(r)
-            pending = []
             if r >= 1 and runs[r - 1][0] != H - 1:
                 multiply(r - 1)
 

@@ -74,8 +74,12 @@ def tile_locallyconnected2d_t_kernel(tc, x, weights, bias, out):
                 taps = valid_taps(h, w)
                 for n, (i, j) in enumerate(taps):
                     row.append((h, w, i, j, n == 0, n == len(taps) - 1))
-            for r0 in range(0, len(row), RUN):
-                runs.append((h, row[r0:r0 + RUN]))
+            if h == 0:
+                for w in range(W):
+                    runs.append((h, [u for u in row if u[1] == w]))
+            else:
+                for r0 in range(0, len(row), RUN):
+                    runs.append((h, row[r0:r0 + RUN]))
         last_use = {}
         for r, (h, units) in enumerate(runs):
             for u in units:
@@ -143,7 +147,7 @@ def tile_locallyconnected2d_t_kernel(tc, x, weights, bias, out):
                 k = state["xbank"]
                 state["xbank"] = k + 1
                 for l in range(2):
-                    if k % 5 in (1, 3):
+                    if k % 3 == 1:
                         nc.vector.tensor_copy(out=dst[:, u0 + 2 * l:u0 + 2 * l + 2, ah, :, :], in_=src[:, l])
                     else:
                         nc.scalar.copy(out=dst[:, u0 + 2 * l:u0 + 2 * l + 2, ah, :, :], in_=src[:, l])
@@ -158,7 +162,7 @@ def tile_locallyconnected2d_t_kernel(tc, x, weights, bias, out):
             elif a + XBUFS == n_chunks:
                 for g in range(WBUFS):
                     load_w(g)
-                    if g == 1:
+                    if g == WBUFS - 1:
                         nc.sync.dma_start(
                             out=bias_sb[:],
                             in_=bias.rearrange("o h w -> (o h w)").partition_broadcast(P))

from contextlib import ExitStack

import concourse.mybir as mybir
from concourse.masks import make_identity

BF16 = mybir.dt.bfloat16
F32 = mybir.dt.float32
U32 = mybir.dt.uint32
U8 = mybir.dt.uint8
FP8X4 = mybir.dt.float8_e4m3fn_x4

P = 128
B, C, O, H, W, KK = 512, 512, 128, 4, 4, 3
S = H * W
TAPS = KK * KK
NBT = B // P
UNIT = 512
UW = 128
RUN = 8

N_VALID = 100
FLOPS = 2 * B * O * C * N_VALID
BYTES = B * C * S * 2 + N_VALID * O * C * 2 + O * S * 2 + B * O * S * 4

XBUFS = 4
WBUFS = 4
SORT_ON_SCALAR = 4
AHEAD = 2


def valid_taps(h, w):
    return [(i, j) for i in range(KK) for j in range(KK)
            if 0 <= h + i - 1 < H and 0 <= w + j - 1 < W]


def tile_locallyconnected2d_t_kernel(tc, x, weights, bias, out):
    nc = tc.nc
    x_rows = x.rearrange("b (z c) h w -> (b z) (c h w)", z=2).rearrange("(a p) e -> a p e", p=P)
    w_rows = weights.rearrange("h w o (z c) i j -> (h w) (o z) (c i j)", z=2).rearrange(
        "g (a p) e -> g p a e", p=P)
    out_rows = out.rearrange("(t p) o h w -> t p (o h w)", p=P)
    n_chunks = x_rows.shape[0]

    with ExitStack() as ctx:
        const = ctx.enter_context(tc.tile_pool(name="const", bufs=1))
        xraw_pool = ctx.enter_context(tc.tile_pool(name="xraw", bufs=XBUFS))
        wraw_pool = ctx.enter_context(tc.tile_pool(name="wraw", bufs=WBUFS))
        work_pool = ctx.enter_context(tc.tile_pool(name="work", bufs=7))
        wq_pool = ctx.enter_context(tc.tile_pool(name="wq", bufs=4))
        tp_pool = ctx.enter_context(tc.psum_pool(name="tp", bufs=4))
        acc_pool = ctx.enter_context(tc.psum_pool(name="acc", bufs=1))
        ctx.enter_context(tc.manual_schedule())

        ident = const.tile([P, P], F32, name="ident")
        make_identity(nc, ident[:])
        x_codes = const.tile([P, NBT * S * UW], U32, name="x_codes", align_bytes=64)
        x_scales = const.tile([P, NBT * S * UW], U8, name="x_scales", align_bytes=64)
        bias_sb = const.tile([P, O * S], BF16, name="bias_sb")
        out_sb = [const.tile([P, O * S], F32, name="out_sb%d" % t) for t in range(NBT)]

        state = {"xbank": 0, "sort": 0}

        def quantise(codes, scales, stage, u0, n, c0):
            nc.vector.quantize_mx(
                out=codes[:, c0:c0 + n * UW].bitcast(FP8X4),
                scales=scales[:, c0:c0 + n * UW],
                in_=stage[:, u0 * UNIT:(u0 + n) * UNIT],
            )

        runs = []
        for h in range(H):
            row = []
            for w in range(W):
                taps = valid_taps(h, w)
                for n, (i, j) in enumerate(taps):
                    row.append((h, w, i, j, n == 0, n == len(taps) - 1))
            if h == 0:
                for w in range(W):
                    runs.append((h, [u for u in row if u[1] == w]))
            else:
                for r0 in range(0, len(row), RUN):
                    runs.append((h, row[r0:r0 + RUN]))
        last_use = {}
        for r, (h, units) in enumerate(runs):
            for u in units:
                last_use[u[0] * W + u[1]] = r

        xraw = {}
        wraw = {}

        def load_x(a):
            t = xraw_pool.tile([P, C // 2 * S], BF16, name="xraw%d" % a, tag="xraw")
            nc.sync.dma_start(out=t[:], in_=x_rows[a])
            xraw[a] = t

        def load_w(g):
            t = wraw_pool.tile([P, 2, C // 2 * TAPS], BF16, name="wraw%d" % g, tag="wraw")
            nc.sync.dma_start(out=t[:], in_=w_rows[g])
            wraw[g] = t

        sorted_w = {}

        def sort_taps(r):
            h, units = runs[r]
            dst = work_pool.tile([P, RUN * UNIT], BF16, name="srt%d" % r, tag="work", align_bytes=64)
            dst_v = dst.rearrange("p (k c) -> p c k", c=UNIT)
            k = 0
            while k < len(units):
                uh, uw, i, j = units[k][:4]
                n = 1
                while k + n < len(units) and units[k + n][:3] == (uh, uw, i):
                    n += 1
                src_v = wraw[uh * W + uw].rearrange("p g (c t) -> p (g c) t", t=TAPS)
                t0 = i * KK + j
                cnt = state["sort"]
                state["sort"] = cnt + 1
                if cnt % SORT_ON_SCALAR == SORT_ON_SCALAR - 1:
                    nc.scalar.copy(out=dst_v[:, :, k:k + n], in_=src_v[:, :, t0:t0 + n])
                else:
                    nc.vector.tensor_copy(out=dst_v[:, :, k:k + n], in_=src_v[:, :, t0:t0 + n])
                k += n
            sorted_w[r] = dst
            for g in range(S):
                if last_use[g] == r and g + WBUFS < S:
                    load_w(g + WBUFS)

        for a in range(XBUFS):
            load_x(a)

        pending = []
        xstage = {}
        for a in range(n_chunks):
            bt, ah = a // 2, a % 2
            words = xraw[a].bitcast(F32).rearrange("p (m k) -> p m k", k=S)
            for q in range(4):
                half, u0 = q // 2, (4 * q) % 8
                if ah == 0 and u0 == 0:
                    xstage[half] = work_pool.tile([P, RUN * UNIT], BF16, name="xst%d_%d" % (bt, half),
                                                  tag="work", align_bytes=64)
                bank = tp_pool.tile([P, UNIT], F32, name="xtp%d_%d" % (a, q), tag="tp")
                for l in range(2):
                    for e in range(2):
                        c0 = (2 * l + e) * P
                        nc.tensor.transpose(bank[:, c0:c0 + P], words[:, :, 8 * e + 2 * q + l], ident[:])
                src = bank.bitcast(BF16).rearrange("p (l e n g) -> p l g n e", l=2, e=2, g=2)
                dst = xstage[half].rearrange("p (u a n e) -> p u a n e", u=8, a=2, e=2)
                k = state["xbank"]
                state["xbank"] = k + 1
                for l in range(2):
                    if k % 3 == 1:
                        nc.vector.tensor_copy(out=dst[:, u0 + 2 * l:u0 + 2 * l + 2, ah, :, :], in_=src[:, l])
                    else:
                        nc.scalar.copy(out=dst[:, u0 + 2 * l:u0 + 2 * l + 2, ah, :, :], in_=src[:, l])
            for job in pending:
                quantise(*job)
            pending = []
            if ah == 1:
                for half in range(2):
                    pending.append((x_codes, x_scales, xstage[half], 0, 8, (bt * S + 8 * half) * UW))
            if a + XBUFS < n_chunks:
                load_x(a + XBUFS)
            elif a + XBUFS == n_chunks:
                for g in range(WBUFS):
                    load_w(g)
                    if g == WBUFS - 1:
                        nc.sync.dma_start(
                            out=bias_sb[:],
                            in_=bias.rearrange("o h w -> (o h w)").partition_broadcast(P))

        sort_taps(0)
        for job in pending:
            quantise(*job)
        sort_taps(1)

        wq = {}
        acc = {}

        def transposes(r):
            h, units = runs[r]
            n = len(units)
            stage = work_pool.tile([P, RUN * UNIT], BF16, name="wst%d" % r, tag="work", align_bytes=64)
            words = sorted_w[r].bitcast(F32)
            stage_w = stage.bitcast(F32)
            for k in range(0, n, 2):
                bank = tp_pool.tile([P, UNIT], F32, name="wtp%d_%d" % (r, k), tag="tp")
                for e in range(4):
                    c0 = (2 * k + e) * P
                    nc.tensor.transpose(bank[:, e * P:(e + 1) * P], words[:, c0:c0 + P], ident[:])
                nc.scalar.copy(out=stage_w[:, k * 256:(k + 2) * 256], in_=bank[:])
            if r + AHEAD < len(runs):
                sort_taps(r + AHEAD)
            codes = wq_pool.tile([P, RUN * UW], U32, name="wc%d" % r, tag="wc", align_bytes=64)
            scales = wq_pool.tile([P, RUN * UW], U8, name="ws%d" % r, tag="ws", align_bytes=64)
            u0 = 0
            for width in (8, 4, 2):
                if n - u0 >= width:
                    quantise(codes, scales, stage, u0, width, u0 * UW)
                    u0 += width
            wq[r] = (codes, scales)

        def passes(h, bt, todo):
            if (h, bt) not in acc:
                acc[(h, bt)] = acc_pool.tile([P, W * O], F32, name="acc%d_%d" % (h, bt), tag="acc%d" % bt)
            bank = acc[(h, bt)]
            for r, k, (uh, uw, i, j, first, last) in todo:
                codes, scales = wq[r]
                s = (uh + i - 1) * W + (uw + j - 1)
                xc = (bt * S + s) * UW
                nc.tensor.matmul_mx(
                    out=bank[:, uw * O:(uw + 1) * O],
                    lhsT=x_codes[:, xc:xc + UW].bitcast(FP8X4),
                    lhsT_scale=x_scales[:, xc:xc + UW],
                    rhs=codes[:, k * UW:(k + 1) * UW].bitcast(FP8X4),
                    rhs_scale=scales[:, k * UW:(k + 1) * UW],
                    start=first,
                    stop=last,
                )

        def finish(h, bt):
            nc.vector.tensor_tensor(
                out=out_sb[bt].rearrange("p (o s) -> p o s", s=S)[:, :, h * W:(h + 1) * W],
                in0=acc[(h, bt)].rearrange("p (w o) -> p o w", w=W),
                in1=bias_sb.rearrange("p (o s) -> p o s", s=S)[:, :, h * W:(h + 1) * W],
                op=mybir.AluOpType.add,
            )

        def multiply(r):
            h, units = runs[r]
            closes = r + 1 == len(runs) or runs[r + 1][0] != h
            todo = [(r, k, u) for k, u in enumerate(units)]
            for bt in range(NBT):
                passes(h, bt, todo)
                if closes:
                    finish(h, bt)

        for r in range(len(runs)):
            transposes(r)
            if r >= 1 and runs[r - 1][0] != H - 1:
                multiply(r - 1)

        todo = [(r, k, u) for r in range(len(runs)) if runs[r][0] == H - 1
                for k, u in enumerate(runs[r][1])]
        for bt in range(NBT):
            passes(H - 1, bt, todo)
            finish(H - 1, bt)
            nc.sync.dma_start(out=out_rows[bt], in_=out_sb[bt][:])
